import numpy as np
import ml_dtypes


def mxq(x, axis, fmt="e4m3"):
    dtype, down = {"e4m3": (ml_dtypes.float8_e4m3fn, 7), "e5m2": (ml_dtypes.float8_e5m2, 14)}[fmt]
    v = np.moveaxis(np.asarray(x, np.float32).astype(ml_dtypes.bfloat16).astype(np.float64), axis, -1)
    blocks = v.reshape(v.shape[:-1] + (-1, 32))
    amax = np.abs(blocks).max(-1, keepdims=True)
    byte = np.maximum(np.where(amax > 0, np.frexp(amax)[1] - 1 + 127, 0) - down, 1)
    scale = np.exp2(byte - 127.0)
    codes = (blocks / scale).astype(np.float32).astype(dtype).astype(np.float64)
    return np.moveaxis((codes * scale).reshape(v.shape), -1, axis)


WIDE = False


def mx_kscale(k):
    if not WIDE:
        return np.ones(k)
    levels = np.array([10, -10, 5, -5, 0])
    a = np.random.permutation(np.resize(levels, k // 512 * 4)).reshape(k // 512, 4)
    idx = np.arange(k)
    return np.exp2(a[idx // 512, idx % 128 // 32])


BF16 = ml_dtypes.bfloat16


def bf(x):
    return np.asarray(x, np.float32).astype(BF16)


def f64(x):
    return np.asarray(x).astype(np.float64)


B, S, DI, DO = 4, 32, 1024, 1024
R = B * S
LN_EPS = 1e-5


def ste_sign(w):
    return np.where(w >= 0, 1.0, -1.0)


def setup_inputs():
    r = np.asarray(mx_kscale(DI), np.float64)[np.arange(R) * DI // R]
    return {"x": bf(np.random.standard_normal((B, S, DI)) * r.reshape(B, S, 1)),
            "weight": bf(np.random.standard_normal((DO, DI)) * 0.02),
            "in_channel_scale": bf(np.random.uniform(0.5, 1.5, DI) / np.sqrt(DI)),
            "out_channel_scale": bf(np.random.uniform(0.5, 1.5, DO) / r.min()),
            "bias": bf(np.random.standard_normal(DO) * 0.3),
            "ln_gamma": bf(1.0 + 0.1 * np.random.standard_normal(DO)),
            "ln_beta": bf(0.1 * np.random.standard_normal(DO))}


def reference(x, weight, in_channel_scale, out_channel_scale, bias, ln_gamma, ln_beta):
    x = f64(x)
    orig_shape = x.shape
    xf = x.reshape(-1, orig_shape[-1])
    w_bin = ste_sign(f64(weight))
    xs = xf * f64(in_channel_scale)
    h = (mxq(xs, 1, "e4m3") @ mxq(w_bin, 1, "e4m3").T) * f64(out_channel_scale)
    h = h + f64(bias)
    mu = np.mean(h, axis=-1, keepdims=True)
    var = np.mean(np.square(h - mu), axis=-1, keepdims=True)
    h = (h - mu) / np.sqrt(var + LN_EPS) * f64(ln_gamma) + f64(ln_beta)
    return h.reshape(*orig_shape[:-1], weight.shape[0])

@@ -1,0 +1,266 @@
+from contextlib import ExitStack
+
+import concourse.mybir as mybir
+from concourse.masks import make_identity
+
+BF16 = mybir.dt.bfloat16
+F32 = mybir.dt.float32
+U32 = mybir.dt.uint32
+U8 = mybir.dt.uint8
+FP8X4 = mybir.dt.float8_e4m3fn_x4
+ALU = mybir.AluOpType
+ACT = mybir.ActivationFunctionType
+
+P = 128
+PACK = 4
+K_PASS = P * PACK
+PAIR = 2
+HALVES = PACK // PAIR
+BANK_F32 = 512
+STATS = 6
+LN_EPS = 1e-5
+
+SIGN_SCALE = 2.0**20
+SIGN_BIAS = 2.0**-120
+
+QUANTISE_LAG = 2
+BACK_LAG = 3
+STATS_LAG = 4
+
+FLOPS = 2 * 128 * 1024 * 1024
+
+
+def tile_onebitlinear_s_kernel(
+    tc, x, weight, in_channel_scale, out_channel_scale, bias, ln_gamma, ln_beta, out
+):
+    nc = tc.nc
+    x_rows = x.flatten_outer_dims()
+    out_rows = out.flatten_outer_dims()
+    d_out, d_in = weight.shape
+    assert x_rows.shape[0] == P
+    passes = d_in // K_PASS
+    chunks = d_out // P
+    banks = d_out // BANK_F32
+    chunks_per_bank = BANK_F32 // P
+    channel_vectors = (out_channel_scale, bias, ln_gamma, ln_beta)
+
+    with ExitStack() as ctx:
+        ctx.enter_context(tc.manual_schedule())
+        keep = ctx.enter_context(tc.tile_pool(name="keep", bufs=1))
+        loads = ctx.enter_context(tc.tile_pool(name="loads", bufs=chunks))
+        signs = ctx.enter_context(tc.tile_pool(name="signs", bufs=3))
+        front = ctx.enter_context(tc.psum_pool(name="front", bufs=3))
+        work = ctx.enter_context(tc.psum_pool(name="work", bufs=2))
+        back = ctx.enter_context(tc.psum_pool(name="back", bufs=1))
+
+        ident_f32 = keep.tile([P, P], F32)
+        make_identity(nc, ident_f32[:])
+        ident_bf16 = keep.tile([P, P], BF16)
+        make_identity(nc, ident_bf16[:])
+        eps_col = keep.tile([P, 1], F32)
+        nc.vector.memset(eps_col[:], LN_EPS)
+        sign_bias_col = keep.tile([P, 1], F32)
+        nc.vector.memset(sign_bias_col[:], SIGN_BIAS)
+        vec_rows = keep.tile([P, P], BF16)
+        nc.vector.memset(vec_rows[:], 0.0)
+
+        w_by_chunk = weight.rearrange("(c p) k -> c p k", p=P)
+        x_sb = keep.tile([P, d_in], BF16)
+        w_chunks = []
+        for c in range(chunks):
+            w_chunk = loads.tile([P, d_in], BF16)
+            nc.sync.dma_start(out=w_chunk[:], in_=w_by_chunk[c])
+            w_chunks.append(w_chunk)
+            if c == 0:
+                nc.sync.dma_start(out=x_sb[:], in_=x_rows)
+
+        ics_cols = keep.tile([P, passes, HALVES, PAIR], BF16)
+        with nc.allow_non_contiguous_dma(reason="512 pieces of 4 bytes, once"):
+            nc.scalar.dma_start(
+                out=ics_cols[:],
+                in_=in_channel_scale.rearrange(
+                    "(g u p e) -> p g u e", g=passes, u=HALVES, e=PAIR
+                ),
+            )
+        for v, vector in enumerate(channel_vectors):
+            nc.scalar.dma_start(
+                out=vec_rows[v * chunks : (v + 1) * chunks, :],
+                in_=vector.rearrange("(c p) -> c p", p=P),
+            )
+        warm = keep.tile([P, 1], F32)
+        nc.scalar.activation(out=warm[:], in_=eps_col[:], func=ACT.Sqrt)
+
+        def transpose_words(src, bank):
+            words = src[:].bitcast(F32)
+            for g in range(passes):
+                for u in range(HALVES):
+                    first = (g * HALVES + u) * P
+                    nc.tensor.transpose(
+                        bank[:, u, g, :], words[:, first : first + P], ident_f32[:]
+                    )
+
+        def as_grouped(bank):
+            return bank[:].bitcast(BF16).rearrange("p u g (r e) -> p g r u e", e=PAIR)
+
+        def grouped_view(tile_ap):
+            return tile_ap.rearrange(
+                "p (g r u e) -> p g r u e", g=passes, u=HALVES, e=PAIR
+            )
+
+        w_banks = {}
+        w_signs = {}
+        products = {}
+        w_codes = keep.tile([P, chunks, passes * P], U32, align_bytes=64)
+        w_scales = keep.tile([P, chunks, passes * P], U8, align_bytes=64)
+        x_codes = keep.tile([P, passes * P], U32, align_bytes=64)
+        x_scales = keep.tile([P, passes * P], U8, align_bytes=64)
+        h_cols = keep.tile([P, chunks, P], F32)
+        stats = keep.tile([P, chunks, STATS], F32)
+        h_banks = []
+        for b in range(banks):
+            h_bank = back.tile([P, chunks_per_bank, P], F32, name="h_bank%d" % b)
+            h_banks.append(h_bank)
+
+        def transpose_weights(c):
+            w_bank = front.tile([P, HALVES, passes, P], F32, tag="front")
+            transpose_words(w_chunks[c], w_bank)
+            w_banks[c] = w_bank
+
+        def take_signs(c):
+            w_sign = signs.tile([P, passes * P * PACK], BF16, align_bytes=64)
+            nc.scalar.activation(
+                out=grouped_view(w_sign[:]),
+                in_=as_grouped(w_banks[c]),
+                func=ACT.Sign,
+                bias=sign_bias_col[:],
+                scale=SIGN_SCALE,
+            )
+            w_signs[c] = w_sign
+
+        def quantise_weights(c):
+            nc.vector.quantize_mx(
+                out=w_codes[:, c, :].bitcast(FP8X4),
+                scales=w_scales[:, c, :],
+                in_=w_signs[c][:],
+            )
+
+        def multiply(c):
+            product = work.tile([P, P], F32, tag="work")
+            for g in range(passes):
+                cols = slice(g * P, (g + 1) * P)
+                nc.tensor.matmul_mx(
+                    out=product[:],
+                    lhsT=w_codes[:, c, cols].bitcast(FP8X4),
+                    lhsT_scale=w_scales[:, c, cols],
+                    rhs=x_codes[:, cols].bitcast(FP8X4),
+                    rhs_scale=x_scales[:, cols],
+                    start=(g == 0),
+                    stop=(g == passes - 1),
+                )
+            products[c] = product
+
+        def scale_and_bias(c):
+            nc.vector.tensor_scalar(
+                out=h_cols[:, c, :],
+                in0=products[c][:],
+                scalar1=chan_cols[:, c : c + 1],
+                scalar2=chan_cols[:, chunks + c : chunks + c + 1],
+                op0=ALU.mult,
+                op1=ALU.add,
+            )
+
+        def transpose_back(c):
+            nc.tensor.transpose(
+                h_banks[c // chunks_per_bank][:, c % chunks_per_bank, :],
+                h_cols[:, c, :],
+                ident_f32[:],
+            )
+
+        def measure(c):
+            nc.vector.bn_stats(
+                out=stats[:, c, :], in_=h_banks[c // chunks_per_bank][:, c % chunks_per_bank, :]
+            )
+
+        norm_rows = []
+        for v in range(2):
+            norm_row = keep.tile([P, d_out], BF16, name="norm_row%d" % v)
+            norm_rows.append(norm_row)
+
+        def spread(v):
+            spread_bank = front.tile([P, chunks, P], BF16, tag="front")
+            for c in range(chunks):
+                col = v * chunks + c
+                nc.tensor.transpose(
+                    spread_bank[:, c, :],
+                    norm_cols[:, col : col + 1].to_broadcast([P, P]),
+                    ident_bf16[:],
+                )
+            nc.scalar.copy(
+                out=norm_rows[v][:], in_=spread_bank[:].rearrange("p c q -> p (c q)")
+            )
+
+        transpose_weights(0)
+        take_signs(0)
+
+        x_bank = work.tile([P, HALVES, passes, P], F32, tag="work")
+        transpose_words(x_sb, x_bank)
+        xs = keep.tile([P, passes * P * PACK], BF16, align_bytes=64)
+        nc.vector.tensor_tensor(
+            out=grouped_view(xs[:]),
+            in0=as_grouped(x_bank),
+            in1=ics_cols[:].unsqueeze(2).to_broadcast([P, passes, P, HALVES, PAIR]),
+            op=ALU.mult,
+        )
+        nc.vector.quantize_mx(out=x_codes[:].bitcast(FP8X4), scales=x_scales[:], in_=xs[:])
+
+        vec_bank = work.tile([P, P], BF16, tag="work")
+        nc.tensor.transpose(vec_bank[:], vec_rows[:], ident_bf16[:])
+        chan_cols = keep.tile([P, 2 * chunks], F32)
+        nc.vector.tensor_copy(out=chan_cols[:], in_=vec_bank[:, 0 : 2 * chunks])
+        norm_cols = keep.tile([P, 2 * chunks], BF16)
+        nc.vector.tensor_copy(out=norm_cols[:], in_=vec_bank[:, 2 * chunks : 4 * chunks])
+
+        for step in range(1, chunks + STATS_LAG):
+            if step < chunks:
+                transpose_weights(step)
+                take_signs(step)
+            elif step < chunks + 2:
+                spread(step - chunks)
+            if 0 <= step - STATS_LAG:
+                measure(step - STATS_LAG)
+            if 0 <= step - BACK_LAG < chunks:
+                scale_and_bias(step - BACK_LAG)
+                transpose_back(step - BACK_LAG)
+            if 0 <= step - QUANTISE_LAG < chunks:
+                quantise_weights(step - QUANTISE_LAG)
+                multiply(step - QUANTISE_LAG)
+
+        mean_var = keep.tile([P, 2], F32)
+        nc.vector.bn_aggr(out=mean_var[:], in_=stats[:].rearrange("p c s -> p (c s)"))
+        std = keep.tile([P, 1], F32)
+        nc.scalar.activation(out=std[:], in_=mean_var[:, 1:2], func=ACT.Sqrt, bias=eps_col[:])
+        centred = keep.tile([P, d_out], F32)
+        for b in range(banks):
+            cols = slice(b * BANK_F32, (b + 1) * BANK_F32)
+            nc.vector.scalar_tensor_tensor(
+                out=centred[:, cols],
+                in0=h_banks[b][:].rearrange("p c q -> p (c q)"),
+                scalar=mean_var[:, 0:1],
+                in1=norm_rows[0][:, cols],
+                op0=ALU.subtract,
+                op1=ALU.mult,
+            )
+        rstd = keep.tile([P, 1], F32)
+        nc.vector.reciprocal(out=rstd[:], in_=std[:])
+        result = keep.tile([P, d_out], F32)
+        for b in range(banks):
+            cols = slice(b * BANK_F32, (b + 1) * BANK_F32)
+            nc.vector.scalar_tensor_tensor(
+                out=result[:, cols],
+                in0=centred[:, cols],
+                scalar=rstd[:],
+                in1=norm_rows[1][:, cols],
+                op0=ALU.mult,
+                op1=ALU.add,
+            )
+            nc.sync.dma_start(out=out_rows[:, cols], in_=result[:, cols])

@@ -42,7 +42,7 @@ def tile_onebitlinear_s_kernel(
     chunks = d_out // P
     banks = d_out // BANK_F32
     chunks_per_bank = BANK_F32 // P
-    channel_vectors = (out_channel_scale, bias, ln_gamma, ln_beta)
+    channel_vectors = (out_channel_scale, bias)
 
     with ExitStack() as ctx:
         ctx.enter_context(tc.manual_schedule())
@@ -73,6 +73,11 @@ def tile_onebitlinear_s_kernel(
             w_chunks.append(w_chunk)
             if c == 0:
                 nc.sync.dma_start(out=x_sb[:], in_=x_rows)
+        norm_rows = []
+        for v, vector in enumerate((ln_gamma, ln_beta)):
+            norm_row = keep.tile([P, d_out], BF16, name="norm_row%d" % v)
+            nc.sync.dma_start(out=norm_row[:], in_=vector.partition_broadcast(P))
+            norm_rows.append(norm_row)
 
         ics_cols = keep.tile([P, passes, HALVES, PAIR], BF16)
         with nc.allow_non_contiguous_dma(reason="512 pieces of 4 bytes, once"):
@@ -181,24 +186,6 @@ def tile_onebitlinear_s_kernel(
                 out=stats[:, c, :], in_=h_banks[c // chunks_per_bank][:, c % chunks_per_bank, :]
             )
 
-        norm_rows = []
-        for v in range(2):
-            norm_row = keep.tile([P, d_out], BF16, name="norm_row%d" % v)
-            norm_rows.append(norm_row)
-
-        def spread(v):
-            spread_bank = front.tile([P, chunks, P], BF16, tag="front")
-            for c in range(chunks):
-                col = v * chunks + c
-                nc.tensor.transpose(
-                    spread_bank[:, c, :],
-                    norm_cols[:, col : col + 1].to_broadcast([P, P]),
-                    ident_bf16[:],
-                )
-            nc.scalar.copy(
-                out=norm_rows[v][:], in_=spread_bank[:].rearrange("p c q -> p (c q)")
-            )
-
         transpose_weights(0)
         take_signs(0)
 
@@ -217,15 +204,11 @@ def tile_onebitlinear_s_kernel(
         nc.tensor.transpose(vec_bank[:], vec_rows[:], ident_bf16[:])
         chan_cols = keep.tile([P, 2 * chunks], F32)
         nc.vector.tensor_copy(out=chan_cols[:], in_=vec_bank[:, 0 : 2 * chunks])
-        norm_cols = keep.tile([P, 2 * chunks], BF16)
-        nc.vector.tensor_copy(out=norm_cols[:], in_=vec_bank[:, 2 * chunks : 4 * chunks])
 
         for step in range(1, chunks + STATS_LAG):
             if step < chunks:
                 transpose_weights(step)
                 take_signs(step)
-            elif step < chunks + 2:
-                spread(step - chunks)
             if 0 <= step - STATS_LAG:
                 measure(step - STATS_LAG)
             if 0 <= step - BACK_LAG < chunks:

@@ -27,6 +27,9 @@ QUANTISE_LAG = 2
 BACK_LAG = 3
 STATS_LAG = 4
 
+VECTOR_CHUNKS = 2
+VECTOR_LEAD = 2
+
 FLOPS = 2 * 128 * 1024 * 1024
 
 
@@ -49,6 +52,7 @@ def tile_onebitlinear_s_kernel(
         keep = ctx.enter_context(tc.tile_pool(name="keep", bufs=1))
         loads = ctx.enter_context(tc.tile_pool(name="loads", bufs=chunks))
         signs = ctx.enter_context(tc.tile_pool(name="signs", bufs=3))
+        early = ctx.enter_context(tc.tile_pool(name="early", bufs=VECTOR_CHUNKS))
         front = ctx.enter_context(tc.psum_pool(name="front", bufs=3))
         work = ctx.enter_context(tc.psum_pool(name="work", bufs=2))
         back = ctx.enter_context(tc.psum_pool(name="back", bufs=1))
@@ -114,6 +118,7 @@ def tile_onebitlinear_s_kernel(
 
         w_banks = {}
         w_signs = {}
+        early_signs = {}
         products = {}
         w_codes = keep.tile([P, chunks, passes * P], U32, align_bytes=64)
         w_scales = keep.tile([P, chunks, passes * P], U8, align_bytes=64)
@@ -126,20 +131,48 @@ def tile_onebitlinear_s_kernel(
             h_bank = back.tile([P, chunks_per_bank, P], F32, name="h_bank%d" % b)
             h_banks.append(h_bank)
 
+        def on_vector(c):
+            return chunks - VECTOR_CHUNKS <= c < chunks
+
+        def compare_on_vector(c):
+            early_sign = early.tile([P, d_in], BF16)
+            nc.vector.tensor_scalar(
+                out=early_sign[:],
+                in0=w_chunks[c][:],
+                scalar1=0.0,
+                scalar2=2.0,
+                op0=ALU.is_ge,
+                op1=ALU.mult,
+            )
+            early_signs[c] = early_sign
+
+        def shift_on_vector(c):
+            nc.vector.tensor_scalar_add(
+                out=early_signs[c][:], in0=early_signs[c][:], scalar1=-1.0
+            )
+
         def transpose_weights(c):
             w_bank = front.tile([P, HALVES, passes, P], F32, tag="front")
-            transpose_words(w_chunks[c], w_bank)
+            transpose_words(early_signs[c] if on_vector(c) else w_chunks[c], w_bank)
             w_banks[c] = w_bank
 
         def take_signs(c):
             w_sign = signs.tile([P, passes * P * PACK], BF16, align_bytes=64)
-            nc.scalar.activation(
-                out=grouped_view(w_sign[:]),
-                in_=as_grouped(w_banks[c]),
-                func=ACT.Sign,
-                bias=sign_bias_col[:],
-                scale=SIGN_SCALE,
-            )
+            if on_vector(c):
+                nc.scalar.copy(
+                    out=w_sign[:]
+                    .bitcast(F32)
+                    .rearrange("p (g r u) -> p g r u", g=passes, u=HALVES),
+                    in_=w_banks[c][:].rearrange("p u g r -> p g r u"),
+                )
+            else:
+                nc.scalar.activation(
+                    out=grouped_view(w_sign[:]),
+                    in_=as_grouped(w_banks[c]),
+                    func=ACT.Sign,
+                    bias=sign_bias_col[:],
+                    scale=SIGN_SCALE,
+                )
             w_signs[c] = w_sign
 
         def quantise_weights(c):
@@ -209,11 +242,15 @@ def tile_onebitlinear_s_kernel(
             if step < chunks:
                 transpose_weights(step)
                 take_signs(step)
+            if on_vector(step + VECTOR_LEAD):
+                compare_on_vector(step + VECTOR_LEAD)
             if 0 <= step - STATS_LAG:
                 measure(step - STATS_LAG)
             if 0 <= step - BACK_LAG < chunks:
                 scale_and_bias(step - BACK_LAG)
                 transpose_back(step - BACK_LAG)
+            if on_vector(step + VECTOR_LEAD):
+                shift_on_vector(step + VECTOR_LEAD)
             if 0 <= step - QUANTISE_LAG < chunks:
                 quantise_weights(step - QUANTISE_LAG)
                 multiply(step - QUANTISE_LAG)

@@ -27,9 +27,6 @@ QUANTISE_LAG = 2
 BACK_LAG = 3
 STATS_LAG = 4
 
-VECTOR_CHUNKS = 2
-VECTOR_LEAD = 2
-
 FLOPS = 2 * 128 * 1024 * 1024
 
 
@@ -52,7 +49,6 @@ def tile_onebitlinear_s_kernel(
         keep = ctx.enter_context(tc.tile_pool(name="keep", bufs=1))
         loads = ctx.enter_context(tc.tile_pool(name="loads", bufs=chunks))
         signs = ctx.enter_context(tc.tile_pool(name="signs", bufs=3))
-        early = ctx.enter_context(tc.tile_pool(name="early", bufs=VECTOR_CHUNKS))
         front = ctx.enter_context(tc.psum_pool(name="front", bufs=3))
         work = ctx.enter_context(tc.psum_pool(name="work", bufs=2))
         back = ctx.enter_context(tc.psum_pool(name="back", bufs=1))
@@ -118,7 +114,6 @@ def tile_onebitlinear_s_kernel(
 
         w_banks = {}
         w_signs = {}
-        early_signs = {}
         products = {}
         w_codes = keep.tile([P, chunks, passes * P], U32, align_bytes=64)
         w_scales = keep.tile([P, chunks, passes * P], U8, align_bytes=64)
@@ -131,48 +126,20 @@ def tile_onebitlinear_s_kernel(
             h_bank = back.tile([P, chunks_per_bank, P], F32, name="h_bank%d" % b)
             h_banks.append(h_bank)
 
-        def on_vector(c):
-            return chunks - VECTOR_CHUNKS <= c < chunks
-
-        def compare_on_vector(c):
-            early_sign = early.tile([P, d_in], BF16)
-            nc.vector.tensor_scalar(
-                out=early_sign[:],
-                in0=w_chunks[c][:],
-                scalar1=0.0,
-                scalar2=2.0,
-                op0=ALU.is_ge,
-                op1=ALU.mult,
-            )
-            early_signs[c] = early_sign
-
-        def shift_on_vector(c):
-            nc.vector.tensor_scalar_add(
-                out=early_signs[c][:], in0=early_signs[c][:], scalar1=-1.0
-            )
-
         def transpose_weights(c):
             w_bank = front.tile([P, HALVES, passes, P], F32, tag="front")
-            transpose_words(early_signs[c] if on_vector(c) else w_chunks[c], w_bank)
+            transpose_words(w_chunks[c], w_bank)
             w_banks[c] = w_bank
 
         def take_signs(c):
             w_sign = signs.tile([P, passes * P * PACK], BF16, align_bytes=64)
-            if on_vector(c):
-                nc.scalar.copy(
-                    out=w_sign[:]
-                    .bitcast(F32)
-                    .rearrange("p (g r u) -> p g r u", g=passes, u=HALVES),
-                    in_=w_banks[c][:].rearrange("p u g r -> p g r u"),
-                )
-            else:
-                nc.scalar.activation(
-                    out=grouped_view(w_sign[:]),
-                    in_=as_grouped(w_banks[c]),
-                    func=ACT.Sign,
-                    bias=sign_bias_col[:],
-                    scale=SIGN_SCALE,
-                )
+            nc.scalar.activation(
+                out=grouped_view(w_sign[:]),
+                in_=as_grouped(w_banks[c]),
+                func=ACT.Sign,
+                bias=sign_bias_col[:],
+                scale=SIGN_SCALE,
+            )
             w_signs[c] = w_sign
 
         def quantise_weights(c):
@@ -242,18 +209,14 @@ def tile_onebitlinear_s_kernel(
             if step < chunks:
                 transpose_weights(step)
                 take_signs(step)
-            if on_vector(step + VECTOR_LEAD):
-                compare_on_vector(step + VECTOR_LEAD)
+            if 0 <= step - QUANTISE_LAG < chunks:
+                quantise_weights(step - QUANTISE_LAG)
+                multiply(step - QUANTISE_LAG)
             if 0 <= step - STATS_LAG:
                 measure(step - STATS_LAG)
             if 0 <= step - BACK_LAG < chunks:
                 scale_and_bias(step - BACK_LAG)
                 transpose_back(step - BACK_LAG)
-            if on_vector(step + VECTOR_LEAD):
-                shift_on_vector(step + VECTOR_LEAD)
-            if 0 <= step - QUANTISE_LAG < chunks:
-                quantise_weights(step - QUANTISE_LAG)
-                multiply(step - QUANTISE_LAG)
 
         mean_var = keep.tile([P, 2], F32)
         nc.vector.bn_aggr(out=mean_var[:], in_=stats[:].rearrange("p c s -> p (c s)"))

@@ -27,6 +27,11 @@ QUANTISE_LAG = 2
 BACK_LAG = 3
 STATS_LAG = 4
 
+VECTOR_CHUNKS = 2
+VECTOR_LEAD = 2
+
+MEASURED = 2
+
 FLOPS = 2 * 128 * 1024 * 1024
 
 
@@ -49,6 +54,7 @@ def tile_onebitlinear_s_kernel(
         keep = ctx.enter_context(tc.tile_pool(name="keep", bufs=1))
         loads = ctx.enter_context(tc.tile_pool(name="loads", bufs=chunks))
         signs = ctx.enter_context(tc.tile_pool(name="signs", bufs=3))
+        early = ctx.enter_context(tc.tile_pool(name="early", bufs=VECTOR_CHUNKS))
         front = ctx.enter_context(tc.psum_pool(name="front", bufs=3))
         work = ctx.enter_context(tc.psum_pool(name="work", bufs=2))
         back = ctx.enter_context(tc.psum_pool(name="back", bufs=1))
@@ -114,32 +120,61 @@ def tile_onebitlinear_s_kernel(
 
         w_banks = {}
         w_signs = {}
+        early_signs = {}
         products = {}
         w_codes = keep.tile([P, chunks, passes * P], U32, align_bytes=64)
         w_scales = keep.tile([P, chunks, passes * P], U8, align_bytes=64)
         x_codes = keep.tile([P, passes * P], U32, align_bytes=64)
         x_scales = keep.tile([P, passes * P], U8, align_bytes=64)
         h_cols = keep.tile([P, chunks, P], F32)
-        stats = keep.tile([P, chunks, STATS], F32)
+        stats = keep.tile([P, chunks // MEASURED, STATS], F32)
         h_banks = []
         for b in range(banks):
             h_bank = back.tile([P, chunks_per_bank, P], F32, name="h_bank%d" % b)
             h_banks.append(h_bank)
 
+        def on_vector(c):
+            return chunks - VECTOR_CHUNKS <= c < chunks
+
+        def compare_on_vector(c):
+            early_sign = early.tile([P, d_in], BF16)
+            nc.vector.tensor_scalar(
+                out=early_sign[:],
+                in0=w_chunks[c][:],
+                scalar1=0.0,
+                scalar2=2.0,
+                op0=ALU.is_ge,
+                op1=ALU.mult,
+            )
+            early_signs[c] = early_sign
+
+        def shift_on_vector(c):
+            nc.vector.tensor_scalar_add(
+                out=early_signs[c][:], in0=early_signs[c][:], scalar1=-1.0
+            )
+
         def transpose_weights(c):
             w_bank = front.tile([P, HALVES, passes, P], F32, tag="front")
-            transpose_words(w_chunks[c], w_bank)
+            transpose_words(early_signs[c] if on_vector(c) else w_chunks[c], w_bank)
             w_banks[c] = w_bank
 
         def take_signs(c):
             w_sign = signs.tile([P, passes * P * PACK], BF16, align_bytes=64)
-            nc.scalar.activation(
-                out=grouped_view(w_sign[:]),
-                in_=as_grouped(w_banks[c]),
-                func=ACT.Sign,
-                bias=sign_bias_col[:],
-                scale=SIGN_SCALE,
-            )
+            if on_vector(c):
+                nc.scalar.copy(
+                    out=w_sign[:]
+                    .bitcast(F32)
+                    .rearrange("p (g r u) -> p g r u", g=passes, u=HALVES),
+                    in_=w_banks[c][:].rearrange("p u g r -> p g r u"),
+                )
+            else:
+                nc.scalar.activation(
+                    out=grouped_view(w_sign[:]),
+                    in_=as_grouped(w_banks[c]),
+                    func=ACT.Sign,
+                    bias=sign_bias_col[:],
+                    scale=SIGN_SCALE,
+                )
             w_signs[c] = w_sign
 
         def quantise_weights(c):
@@ -182,8 +217,10 @@ def tile_onebitlinear_s_kernel(
             )
 
         def measure(c):
+            last = c % chunks_per_bank
             nc.vector.bn_stats(
-                out=stats[:, c, :], in_=h_banks[c // chunks_per_bank][:, c % chunks_per_bank, :]
+                out=stats[:, c // MEASURED, :],
+                in_=h_banks[c // chunks_per_bank][:, last + 1 - MEASURED : last + 1, :],
             )
 
         transpose_weights(0)
@@ -212,11 +249,15 @@ def tile_onebitlinear_s_kernel(
             if 0 <= step - QUANTISE_LAG < chunks:
                 quantise_weights(step - QUANTISE_LAG)
                 multiply(step - QUANTISE_LAG)
-            if 0 <= step - STATS_LAG:
+            if on_vector(step + VECTOR_LEAD):
+                compare_on_vector(step + VECTOR_LEAD)
+            if 0 <= step - STATS_LAG and (step - STATS_LAG) % MEASURED == MEASURED - 1:
                 measure(step - STATS_LAG)
             if 0 <= step - BACK_LAG < chunks:
                 scale_and_bias(step - BACK_LAG)
                 transpose_back(step - BACK_LAG)
+            if on_vector(step + VECTOR_LEAD):
+                shift_on_vector(step + VECTOR_LEAD)
 
         mean_var = keep.tile([P, 2], F32)
         nc.vector.bn_aggr(out=mean_var[:], in_=stats[:].rearrange("p c s -> p (c s)"))

@@ -47,7 +47,6 @@ def tile_onebitlinear_s_kernel(
     chunks = d_out // P
     banks = d_out // BANK_F32
     chunks_per_bank = BANK_F32 // P
-    channel_vectors = (out_channel_scale, bias)
 
     with ExitStack() as ctx:
         ctx.enter_context(tc.manual_schedule())
@@ -61,16 +60,12 @@ def tile_onebitlinear_s_kernel(
 
         ident_f32 = keep.tile([P, P], F32)
         make_identity(nc, ident_f32[:])
-        ident_bf16 = keep.tile([P, P], BF16)
-        make_identity(nc, ident_bf16[:])
         eps_col = keep.tile([P, 1], F32)
         nc.vector.memset(eps_col[:], LN_EPS)
         sign_bias_col = keep.tile([P, 1], F32)
         nc.vector.memset(sign_bias_col[:], SIGN_BIAS)
-        vec_rows = keep.tile([P, P], BF16)
-        nc.vector.memset(vec_rows[:], 0.0)
 
-        w_by_chunk = weight.rearrange("(c p) k -> c p k", p=P)
+        w_by_chunk = weight.rearrange("(p c) k -> c p k", p=P)
         x_sb = keep.tile([P, d_in], BF16)
         w_chunks = []
         for c in range(chunks):
@@ -93,11 +88,13 @@ def tile_onebitlinear_s_kernel(
                     "(g u p e) -> p g u e", g=passes, u=HALVES, e=PAIR
                 ),
             )
-        for v, vector in enumerate(channel_vectors):
+        chan_cols = []
+        for v, vector in enumerate((out_channel_scale, bias)):
+            chan_col = keep.tile([P, chunks], BF16, name="chan_col%d" % v)
             nc.scalar.dma_start(
-                out=vec_rows[v * chunks : (v + 1) * chunks, :],
-                in_=vector.rearrange("(c p) -> c p", p=P),
+                out=chan_col[:], in_=vector.rearrange("(p c) -> p c", c=chunks)
             )
+            chan_cols.append(chan_col)
         warm = keep.tile([P, 1], F32)
         nc.scalar.activation(out=warm[:], in_=eps_col[:], func=ACT.Sqrt)
 
@@ -203,8 +200,8 @@ def tile_onebitlinear_s_kernel(
             nc.vector.tensor_scalar(
                 out=h_cols[:, c, :],
                 in0=products[c][:],
-                scalar1=chan_cols[:, c : c + 1],
-                scalar2=chan_cols[:, chunks + c : chunks + c + 1],
+                scalar1=chan_cols[0][:, c : c + 1],
+                scalar2=chan_cols[1][:, c : c + 1],
                 op0=ALU.mult,
                 op1=ALU.add,
             )
@@ -237,11 +234,6 @@ def tile_onebitlinear_s_kernel(
         )
         nc.vector.quantize_mx(out=x_codes[:].bitcast(FP8X4), scales=x_scales[:], in_=xs[:])
 
-        vec_bank = work.tile([P, P], BF16, tag="work")
-        nc.tensor.transpose(vec_bank[:], vec_rows[:], ident_bf16[:])
-        chan_cols = keep.tile([P, 2 * chunks], F32)
-        nc.vector.tensor_copy(out=chan_cols[:], in_=vec_bank[:, 0 : 2 * chunks])
-
         for step in range(1, chunks + STATS_LAG):
             if step < chunks:
                 transpose_weights(step)
@@ -265,12 +257,12 @@ def tile_onebitlinear_s_kernel(
         nc.scalar.activation(out=std[:], in_=mean_var[:, 1:2], func=ACT.Sqrt, bias=eps_col[:])
         centred = keep.tile([P, d_out], F32)
         for b in range(banks):
-            cols = slice(b * BANK_F32, (b + 1) * BANK_F32)
+            held = slice(b * chunks_per_bank, (b + 1) * chunks_per_bank)
             nc.vector.scalar_tensor_tensor(
-                out=centred[:, cols],
-                in0=h_banks[b][:].rearrange("p c q -> p (c q)"),
+                out=centred[:].rearrange("p (q c) -> p q c", c=chunks)[:, :, held],
+                in0=h_banks[b][:].rearrange("p c q -> p q c"),
                 scalar=mean_var[:, 0:1],
-                in1=norm_rows[0][:, cols],
+                in1=norm_rows[0][:].rearrange("p (q c) -> p q c", c=chunks)[:, :, held],
                 op0=ALU.subtract,
                 op1=ALU.mult,
             )

@@ -23,14 +23,12 @@ LN_EPS = 1e-5
 SIGN_SCALE = 2.0**20
 SIGN_BIAS = 2.0**-120
 
-QUANTISE_LAG = 2
-BACK_LAG = 3
-STATS_LAG = 4
-
-VECTOR_CHUNKS = 2
-VECTOR_LEAD = 2
+VECTOR_CHUNKS = (1, 5)
+X_CHUNK = 3
 
 MEASURED = 2
+ALONE = 2
+PARTS = ((0, 4), (4, 3), (7, 1))
 
 FLOPS = 2 * 128 * 1024 * 1024
 
@@ -46,39 +44,26 @@ def tile_onebitlinear_s_kernel(
     passes = d_in // K_PASS
     chunks = d_out // P
     banks = d_out // BANK_F32
-    chunks_per_bank = BANK_F32 // P
 
     with ExitStack() as ctx:
         ctx.enter_context(tc.manual_schedule())
         keep = ctx.enter_context(tc.tile_pool(name="keep", bufs=1))
         loads = ctx.enter_context(tc.tile_pool(name="loads", bufs=chunks))
-        signs = ctx.enter_context(tc.tile_pool(name="signs", bufs=3))
-        early = ctx.enter_context(tc.tile_pool(name="early", bufs=VECTOR_CHUNKS))
-        front = ctx.enter_context(tc.psum_pool(name="front", bufs=3))
+        signs = ctx.enter_context(tc.tile_pool(name="signs", bufs=chunks))
+        front = ctx.enter_context(tc.psum_pool(name="front", bufs=4))
         work = ctx.enter_context(tc.psum_pool(name="work", bufs=2))
-        back = ctx.enter_context(tc.psum_pool(name="back", bufs=1))
+        back = ctx.enter_context(tc.psum_pool(name="back", bufs=2))
 
         ident_f32 = keep.tile([P, P], F32)
         make_identity(nc, ident_f32[:])
+        ident_bf16 = keep.tile([P, P], BF16)
+        make_identity(nc, ident_bf16[:])
+        vec_rows = keep.tile([P, P], BF16)
+        nc.vector.memset(vec_rows[:], 0.0)
         eps_col = keep.tile([P, 1], F32)
         nc.vector.memset(eps_col[:], LN_EPS)
         sign_bias_col = keep.tile([P, 1], F32)
         nc.vector.memset(sign_bias_col[:], SIGN_BIAS)
-
-        w_by_chunk = weight.rearrange("(p c) k -> c p k", p=P)
-        x_sb = keep.tile([P, d_in], BF16)
-        w_chunks = []
-        for c in range(chunks):
-            w_chunk = loads.tile([P, d_in], BF16)
-            nc.sync.dma_start(out=w_chunk[:], in_=w_by_chunk[c])
-            w_chunks.append(w_chunk)
-            if c == 0:
-                nc.sync.dma_start(out=x_sb[:], in_=x_rows)
-        norm_rows = []
-        for v, vector in enumerate((ln_gamma, ln_beta)):
-            norm_row = keep.tile([P, d_out], BF16, name="norm_row%d" % v)
-            nc.sync.dma_start(out=norm_row[:], in_=vector.partition_broadcast(P))
-            norm_rows.append(norm_row)
 
         ics_cols = keep.tile([P, passes, HALVES, PAIR], BF16)
         with nc.allow_non_contiguous_dma(reason="512 pieces of 4 bytes, once"):
@@ -88,15 +73,31 @@ def tile_onebitlinear_s_kernel(
                     "(g u p e) -> p g u e", g=passes, u=HALVES, e=PAIR
                 ),
             )
-        chan_cols = []
         for v, vector in enumerate((out_channel_scale, bias)):
-            chan_col = keep.tile([P, chunks], BF16, name="chan_col%d" % v)
             nc.scalar.dma_start(
-                out=chan_col[:], in_=vector.rearrange("(p c) -> p c", c=chunks)
+                out=vec_rows[v * chunks : (v + 1) * chunks, :],
+                in_=vector.rearrange("(c p) -> c p", p=P),
             )
-            chan_cols.append(chan_col)
         warm = keep.tile([P, 1], F32)
         nc.scalar.activation(out=warm[:], in_=eps_col[:], func=ACT.Sqrt)
+
+        w_by_chunk = weight.rearrange("(c p) k -> c p k", p=P)
+        x_sb = keep.tile([P, d_in], BF16)
+        w_chunks = []
+        for c in range(chunks):
+            if c == X_CHUNK:
+                nc.sync.dma_start(out=x_sb[:], in_=x_rows)
+            w_chunk = loads.tile([P, d_in], BF16)
+            pieces = passes if c == 0 else 1
+            for i in range(pieces):
+                cols = slice(i * d_in // pieces, (i + 1) * d_in // pieces)
+                nc.sync.dma_start(out=w_chunk[:, cols], in_=w_by_chunk[c][:, cols])
+            w_chunks.append(w_chunk)
+        norm_rows = []
+        for v, vector in enumerate((ln_gamma, ln_beta)):
+            norm_row = keep.tile([P, d_out], BF16, name="norm_row%d" % v)
+            nc.sync.dma_start(out=norm_row[:], in_=vector.partition_broadcast(P))
+            norm_rows.append(norm_row)
 
         def transpose_words(src, bank):
             words = src[:].bitcast(F32)
@@ -117,76 +118,75 @@ def tile_onebitlinear_s_kernel(
 
         w_banks = {}
         w_signs = {}
-        early_signs = {}
         products = {}
         w_codes = keep.tile([P, chunks, passes * P], U32, align_bytes=64)
         w_scales = keep.tile([P, chunks, passes * P], U8, align_bytes=64)
         x_codes = keep.tile([P, passes * P], U32, align_bytes=64)
         x_scales = keep.tile([P, passes * P], U8, align_bytes=64)
+        xs = keep.tile([P, passes * P * PACK], BF16, align_bytes=64)
         h_cols = keep.tile([P, chunks, P], F32)
-        stats = keep.tile([P, chunks // MEASURED, STATS], F32)
-        h_banks = []
-        for b in range(banks):
-            h_bank = back.tile([P, chunks_per_bank, P], F32, name="h_bank%d" % b)
-            h_banks.append(h_bank)
-
-        def on_vector(c):
-            return chunks - VECTOR_CHUNKS <= c < chunks
-
-        def compare_on_vector(c):
-            early_sign = early.tile([P, d_in], BF16)
-            nc.vector.tensor_scalar(
-                out=early_sign[:],
-                in0=w_chunks[c][:],
-                scalar1=0.0,
-                scalar2=2.0,
-                op0=ALU.is_ge,
-                op1=ALU.mult,
-            )
-            early_signs[c] = early_sign
-
-        def shift_on_vector(c):
-            nc.vector.tensor_scalar_add(
-                out=early_signs[c][:], in0=early_signs[c][:], scalar1=-1.0
-            )
+        stats = keep.tile([P, len(PARTS), STATS], F32)
+        h_parts = {}
+        both = slice(0, passes)
 
         def transpose_weights(c):
             w_bank = front.tile([P, HALVES, passes, P], F32, tag="front")
-            transpose_words(early_signs[c] if on_vector(c) else w_chunks[c], w_bank)
+            transpose_words(w_chunks[c], w_bank)
             w_banks[c] = w_bank
-
-        def take_signs(c):
             w_sign = signs.tile([P, passes * P * PACK], BF16, align_bytes=64)
-            if on_vector(c):
-                nc.scalar.copy(
-                    out=w_sign[:]
-                    .bitcast(F32)
-                    .rearrange("p (g r u) -> p g r u", g=passes, u=HALVES),
-                    in_=w_banks[c][:].rearrange("p u g r -> p g r u"),
-                )
-            else:
+            w_signs[c] = w_sign
+
+        def sign_on_scalar(c, pieces=1):
+            for i in range(pieces):
+                held = slice(i * passes // pieces, (i + 1) * passes // pieces)
                 nc.scalar.activation(
-                    out=grouped_view(w_sign[:]),
-                    in_=as_grouped(w_banks[c]),
+                    out=grouped_view(w_signs[c][:])[:, held],
+                    in_=as_grouped(w_banks[c])[:, held],
                     func=ACT.Sign,
                     bias=sign_bias_col[:],
                     scale=SIGN_SCALE,
                 )
-            w_signs[c] = w_sign
 
-        def quantise_weights(c):
-            nc.vector.quantize_mx(
-                out=w_codes[:, c, :].bitcast(FP8X4),
-                scales=w_scales[:, c, :],
-                in_=w_signs[c][:],
+        def compare_on_vector(c):
+            nc.vector.tensor_scalar(
+                out=grouped_view(w_signs[c][:]),
+                in0=as_grouped(w_banks[c]),
+                scalar1=0.0,
+                scalar2=0.5,
+                op0=ALU.is_ge,
+                op1=ALU.subtract,
             )
 
-        def multiply(c):
-            product = work.tile([P, P], F32, tag="work")
-            for g in range(passes):
+        def double_on_vector(c):
+            nc.vector.tensor_scalar_mul(out=w_signs[c][:], in0=w_signs[c][:], scalar1=2.0)
+
+        def leave(c, pieces=1):
+            if c in VECTOR_CHUNKS:
+                compare_on_vector(c)
+            else:
+                sign_on_scalar(c, pieces)
+
+        def quantise_weights(c, gs=both):
+            cols = slice(gs.start * P, gs.stop * P)
+            nc.vector.quantize_mx(
+                out=w_codes[:, c, cols].bitcast(FP8X4),
+                scales=w_scales[:, c, cols],
+                in_=w_signs[c][:, gs.start * P * PACK : gs.stop * P * PACK],
+            )
+
+        def multiply(c, gs=both):
+            if c not in products:
+                if c >= chunks - ALONE:
+                    product_bank = front.tile([P, P], F32, tag="front")
+                    products[c] = product_bank[:]
+                else:
+                    pair_bank = work.tile([P, MEASURED, P], F32, tag="work")
+                    for i in range(MEASURED):
+                        products[c + i] = pair_bank[:, i, :]
+            for g in range(gs.start, gs.stop):
                 cols = slice(g * P, (g + 1) * P)
                 nc.tensor.matmul_mx(
-                    out=product[:],
+                    out=products[c],
                     lhsT=w_codes[:, c, cols].bitcast(FP8X4),
                     lhsT_scale=w_scales[:, c, cols],
                     rhs=x_codes[:, cols].bitcast(FP8X4),
@@ -194,75 +194,117 @@ def tile_onebitlinear_s_kernel(
                     start=(g == 0),
                     stop=(g == passes - 1),
                 )
-            products[c] = product
 
-        def scale_and_bias(c):
-            nc.vector.tensor_scalar(
-                out=h_cols[:, c, :],
-                in0=products[c][:],
-                scalar1=chan_cols[0][:, c : c + 1],
-                scalar2=chan_cols[1][:, c : c + 1],
-                op0=ALU.mult,
-                op1=ALU.add,
-            )
+        def finish(c):
+            scale_col = chan_cols[:, c : c + 1]
+            bias_col = chan_cols[:, chunks + c : chunks + c + 1]
+            if c >= chunks - ALONE:
+                nc.scalar.activation(
+                    out=h_cols[:, c, :],
+                    in_=products[c],
+                    func=ACT.Identity,
+                    bias=bias_col,
+                    scale=scale_col,
+                )
+            else:
+                nc.vector.tensor_scalar(
+                    out=h_cols[:, c, :],
+                    in0=products[c],
+                    scalar1=scale_col,
+                    scalar2=bias_col,
+                    op0=ALU.mult,
+                    op1=ALU.add,
+                )
+            for first, width in PARTS:
+                if first <= c < first + width:
+                    if c == first:
+                        h_part = (front if width == 1 else back).tile(
+                            [P, width, P], F32, name="h_part%d" % first, tag="front" if width == 1 else "back"
+                        )
+                        h_parts[first] = h_part
+                    nc.tensor.transpose(
+                        h_parts[first][:, c - first, :], h_cols[:, c, :], ident_f32[:]
+                    )
 
-        def transpose_back(c):
-            nc.tensor.transpose(
-                h_banks[c // chunks_per_bank][:, c % chunks_per_bank, :],
-                h_cols[:, c, :],
-                ident_f32[:],
-            )
-
-        def measure(c):
-            last = c % chunks_per_bank
+        def measure(i):
+            first, width = PARTS[i]
             nc.vector.bn_stats(
-                out=stats[:, c // MEASURED, :],
-                in_=h_banks[c // chunks_per_bank][:, last + 1 - MEASURED : last + 1, :],
+                out=stats[:, i, :], in_=h_parts[first][:].rearrange("p c q -> p (c q)")
             )
 
         transpose_weights(0)
-        take_signs(0)
-
+        leave(0)
+        transpose_weights(1)
+        leave(1)
+        transpose_weights(2)
+        leave(2)
         x_bank = work.tile([P, HALVES, passes, P], F32, tag="work")
         transpose_words(x_sb, x_bank)
-        xs = keep.tile([P, passes * P * PACK], BF16, align_bytes=64)
+        quantise_weights(0)
+        double_on_vector(1)
         nc.vector.tensor_tensor(
             out=grouped_view(xs[:]),
             in0=as_grouped(x_bank),
             in1=ics_cols[:].unsqueeze(2).to_broadcast([P, passes, P, HALVES, PAIR]),
             op=ALU.mult,
         )
+        transpose_weights(3)
+        leave(3)
+        quantise_weights(1)
         nc.vector.quantize_mx(out=x_codes[:].bitcast(FP8X4), scales=x_scales[:], in_=xs[:])
-
-        for step in range(1, chunks + STATS_LAG):
-            if step < chunks:
-                transpose_weights(step)
-                take_signs(step)
-            if 0 <= step - QUANTISE_LAG < chunks:
-                quantise_weights(step - QUANTISE_LAG)
-                multiply(step - QUANTISE_LAG)
-            if on_vector(step + VECTOR_LEAD):
-                compare_on_vector(step + VECTOR_LEAD)
-            if 0 <= step - STATS_LAG and (step - STATS_LAG) % MEASURED == MEASURED - 1:
-                measure(step - STATS_LAG)
-            if 0 <= step - BACK_LAG < chunks:
-                scale_and_bias(step - BACK_LAG)
-                transpose_back(step - BACK_LAG)
-            if on_vector(step + VECTOR_LEAD):
-                shift_on_vector(step + VECTOR_LEAD)
+        vec_bank = work.tile([P, P], BF16, tag="work")
+        nc.tensor.transpose(vec_bank[:], vec_rows[:], ident_bf16[:])
+        chan_cols = keep.tile([P, 2 * chunks], F32)
+        nc.vector.tensor_copy(out=chan_cols[:], in_=vec_bank[:, 0 : 2 * chunks])
+        transpose_weights(4)
+        leave(4)
+        quantise_weights(2)
+        transpose_weights(5)
+        leave(5)
+        quantise_weights(3)
+        double_on_vector(5)
+        transpose_weights(6)
+        leave(6)
+        multiply(0)
+        multiply(1)
+        multiply(2)
+        transpose_weights(7)
+        leave(7, passes)
+        quantise_weights(4)
+        multiply(3)
+        quantise_weights(5)
+        finish(0)
+        finish(1)
+        multiply(4)
+        multiply(5)
+        quantise_weights(6)
+        finish(2)
+        finish(3)
+        multiply(6)
+        quantise_weights(7, slice(0, 1))
+        multiply(7, slice(0, 1))
+        finish(4)
+        finish(5)
+        quantise_weights(7, slice(1, passes))
+        multiply(7, slice(1, passes))
+        measure(0)
+        finish(6)
+        finish(7)
+        measure(1)
+        measure(2)
 
         mean_var = keep.tile([P, 2], F32)
         nc.vector.bn_aggr(out=mean_var[:], in_=stats[:].rearrange("p c s -> p (c s)"))
         std = keep.tile([P, 1], F32)
         nc.scalar.activation(out=std[:], in_=mean_var[:, 1:2], func=ACT.Sqrt, bias=eps_col[:])
         centred = keep.tile([P, d_out], F32)
-        for b in range(banks):
-            held = slice(b * chunks_per_bank, (b + 1) * chunks_per_bank)
+        for first, width in PARTS:
+            cols = slice(first * P, (first + width) * P)
             nc.vector.scalar_tensor_tensor(
-                out=centred[:].rearrange("p (q c) -> p q c", c=chunks)[:, :, held],
-                in0=h_banks[b][:].rearrange("p c q -> p q c"),
+                out=centred[:, cols],
+                in0=h_parts[first][:].rearrange("p c q -> p (c q)"),
                 scalar=mean_var[:, 0:1],
-                in1=norm_rows[0][:].rearrange("p (q c) -> p q c", c=chunks)[:, :, held],
+                in1=norm_rows[0][:, cols],
                 op0=ALU.subtract,
                 op1=ALU.mult,
             )

@@ -16,7 +16,6 @@ PACK = 4
 K_PASS = P * PACK
 PAIR = 2
 HALVES = PACK // PAIR
-BANK_F32 = 512
 STATS = 6
 LN_EPS = 1e-5
 
@@ -26,8 +25,8 @@ SIGN_BIAS = 2.0**-120
 VECTOR_CHUNKS = (1, 5)
 X_CHUNK = 3
 
-MEASURED = 2
-ALONE = 2
+BANKS_OF_PRODUCTS = {0: 2, 2: 2, 4: 3, 7: 1}
+SCALAR_SCALES = 4
 PARTS = ((0, 4), (4, 3), (7, 1))
 
 FLOPS = 2 * 128 * 1024 * 1024
@@ -43,7 +42,6 @@ def tile_onebitlinear_s_kernel(
     assert x_rows.shape[0] == P
     passes = d_in // K_PASS
     chunks = d_out // P
-    banks = d_out // BANK_F32
 
     with ExitStack() as ctx:
         ctx.enter_context(tc.manual_schedule())
@@ -175,14 +173,12 @@ def tile_onebitlinear_s_kernel(
             )
 
         def multiply(c, gs=both):
-            if c not in products:
-                if c >= chunks - ALONE:
-                    product_bank = front.tile([P, P], F32, tag="front")
-                    products[c] = product_bank[:]
-                else:
-                    pair_bank = work.tile([P, MEASURED, P], F32, tag="work")
-                    for i in range(MEASURED):
-                        products[c + i] = pair_bank[:, i, :]
+            if c in BANKS_OF_PRODUCTS and gs.start == 0:
+                held = BANKS_OF_PRODUCTS[c]
+                pool, tag = (front, "front") if held > 2 else (work, "work")
+                bank = pool.tile([P, held, P], F32, name="products%d" % c, tag=tag)
+                for i in range(held):
+                    products[c + i] = bank[:, i, :]
             for g in range(gs.start, gs.stop):
                 cols = slice(g * P, (g + 1) * P)
                 nc.tensor.matmul_mx(
@@ -195,10 +191,10 @@ def tile_onebitlinear_s_kernel(
                     stop=(g == passes - 1),
                 )
 
-        def finish(c):
+        def scale(c):
             scale_col = chan_cols[:, c : c + 1]
             bias_col = chan_cols[:, chunks + c : chunks + c + 1]
-            if c >= chunks - ALONE:
+            if c >= SCALAR_SCALES:
                 nc.scalar.activation(
                     out=h_cols[:, c, :],
                     in_=products[c],
@@ -215,6 +211,7 @@ def tile_onebitlinear_s_kernel(
                     op0=ALU.mult,
                     op1=ALU.add,
                 )
+        def transpose_back(c):
             for first, width in PARTS:
                 if first <= c < first + width:
                     if c == first:
@@ -272,24 +269,32 @@ def tile_onebitlinear_s_kernel(
         leave(7, passes)
         quantise_weights(4)
         multiply(3)
-        quantise_weights(5)
-        finish(0)
-        finish(1)
         multiply(4)
+        quantise_weights(5)
         multiply(5)
+        scale(0)
+        scale(1)
+        transpose_back(0)
+        transpose_back(1)
         quantise_weights(6)
-        finish(2)
-        finish(3)
         multiply(6)
+        scale(2)
+        scale(3)
+        transpose_back(2)
+        transpose_back(3)
         quantise_weights(7, slice(0, 1))
         multiply(7, slice(0, 1))
-        finish(4)
-        finish(5)
+        scale(4)
+        scale(5)
+        scale(6)
         quantise_weights(7, slice(1, passes))
         multiply(7, slice(1, passes))
         measure(0)
-        finish(6)
-        finish(7)
+        transpose_back(4)
+        transpose_back(5)
+        transpose_back(6)
+        scale(7)
+        transpose_back(7)
         measure(1)
         measure(2)
 
@@ -297,6 +302,7 @@ def tile_onebitlinear_s_kernel(
         nc.vector.bn_aggr(out=mean_var[:], in_=stats[:].rearrange("p c s -> p (c s)"))
         std = keep.tile([P, 1], F32)
         nc.scalar.activation(out=std[:], in_=mean_var[:, 1:2], func=ACT.Sqrt, bias=eps_col[:])
+        rstd = keep.tile([P, 1], F32)
         centred = keep.tile([P, d_out], F32)
         for first, width in PARTS:
             cols = slice(first * P, (first + width) * P)
@@ -308,11 +314,11 @@ def tile_onebitlinear_s_kernel(
                 op0=ALU.subtract,
                 op1=ALU.mult,
             )
-        rstd = keep.tile([P, 1], F32)
-        nc.vector.reciprocal(out=rstd[:], in_=std[:])
+            if first == 0:
+                nc.vector.reciprocal(out=rstd[:], in_=std[:])
         result = keep.tile([P, d_out], F32)
-        for b in range(banks):
-            cols = slice(b * BANK_F32, (b + 1) * BANK_F32)
+        for first, width in PARTS:
+            cols = slice(first * P, (first + width) * P)
             nc.vector.scalar_tensor_tensor(
                 out=result[:, cols],
                 in0=centred[:, cols],

@@ -27,6 +27,8 @@ X_CHUNK = 3
 
 BANKS_OF_PRODUCTS = {0: 2, 2: 2, 4: 3, 7: 1}
 SCALAR_SCALES = 4
+WARM_UPS = 12
+
 PARTS = ((0, 4), (4, 3), (7, 1))
 
 FLOPS = 2 * 128 * 1024 * 1024
@@ -228,6 +230,10 @@ def tile_onebitlinear_s_kernel(
             nc.vector.bn_stats(
                 out=stats[:, i, :], in_=h_parts[first][:].rearrange("p c q -> p (c q)")
             )
+
+        warm_bank = back.tile([P, P], F32, name="warm_bank", tag="back")
+        for i in range(WARM_UPS):
+            nc.tensor.transpose(warm_bank[:], ident_f32[:], ident_f32[:])
 
         transpose_weights(0)
         leave(0)

@@ -73,7 +73,7 @@ def tile_onebitlinear_s_kernel(
                     "(g u p e) -> p g u e", g=passes, u=HALVES, e=PAIR
                 ),
             )
-        for v, vector in enumerate((out_channel_scale, bias)):
+        for v, vector in enumerate((out_channel_scale, bias, ln_beta)):
             nc.scalar.dma_start(
                 out=vec_rows[v * chunks : (v + 1) * chunks, :],
                 in_=vector.rearrange("(c p) -> c p", p=P),
@@ -93,11 +93,8 @@ def tile_onebitlinear_s_kernel(
                 cols = slice(i * d_in // pieces, (i + 1) * d_in // pieces)
                 nc.sync.dma_start(out=w_chunk[:, cols], in_=w_by_chunk[c][:, cols])
             w_chunks.append(w_chunk)
-        norm_rows = []
-        for v, vector in enumerate((ln_gamma, ln_beta)):
-            norm_row = keep.tile([P, d_out], BF16, name="norm_row%d" % v)
-            nc.sync.dma_start(out=norm_row[:], in_=vector.partition_broadcast(P))
-            norm_rows.append(norm_row)
+        gamma_rows = keep.tile([P, d_out], BF16)
+        nc.sync.dma_start(out=gamma_rows[:], in_=ln_gamma.partition_broadcast(P))
 
         def transpose_words(src, bank):
             words = src[:].bitcast(F32)
@@ -259,6 +256,8 @@ def tile_onebitlinear_s_kernel(
         nc.tensor.transpose(vec_bank[:], vec_rows[:], ident_bf16[:])
         chan_cols = keep.tile([P, 2 * chunks], F32)
         nc.vector.tensor_copy(out=chan_cols[:], in_=vec_bank[:, 0 : 2 * chunks])
+        beta_cols = keep.tile([P, chunks], BF16)
+        nc.vector.tensor_copy(out=beta_cols[:], in_=vec_bank[:, 2 * chunks : 3 * chunks])
         transpose_weights(4)
         leave(4)
         quantise_weights(2)
@@ -301,6 +300,11 @@ def tile_onebitlinear_s_kernel(
         transpose_back(6)
         scale(7)
         transpose_back(7)
+        beta_rows = front.tile([P, chunks, P], BF16, name="beta_rows", tag="front")
+        for c in range(chunks):
+            nc.tensor.transpose(
+                beta_rows[:, c, :], beta_cols[:, c : c + 1].to_broadcast([P, P]), ident_bf16[:]
+            )
         measure(1)
         measure(2)
 
@@ -316,7 +320,7 @@ def tile_onebitlinear_s_kernel(
                 out=centred[:, cols],
                 in0=h_parts[first][:].rearrange("p c q -> p (c q)"),
                 scalar=mean_var[:, 0:1],
-                in1=norm_rows[0][:, cols],
+                in1=gamma_rows[:, cols],
                 op0=ALU.subtract,
                 op1=ALU.mult,
             )
@@ -329,7 +333,7 @@ def tile_onebitlinear_s_kernel(
                 out=result[:, cols],
                 in0=centred[:, cols],
                 scalar=rstd[:],
-                in1=norm_rows[1][:, cols],
+                in1=beta_rows[:].rearrange("p c q -> p (c q)")[:, cols],
                 op0=ALU.mult,
                 op1=ALU.add,
             )

@@ -23,13 +23,14 @@ SIGN_SCALE = 2.0**20
 SIGN_BIAS = 2.0**-120
 
 VECTOR_CHUNKS = (1, 5)
-X_CHUNK = 3
+X_CHUNK = 4
 
 BANKS_OF_PRODUCTS = {0: 2, 2: 2, 4: 3, 7: 1}
 SCALAR_SCALES = 4
-WARM_UPS = 12
+WARM_UPS = 2
+WARM_COLUMNS = 256
 
-PARTS = ((0, 4), (4, 3), (7, 1))
+PARTS = ((0, 4), (4, 2), (6, 2))
 
 FLOPS = 2 * 128 * 1024 * 1024
 
@@ -54,6 +55,8 @@ def tile_onebitlinear_s_kernel(
         work = ctx.enter_context(tc.psum_pool(name="work", bufs=2))
         back = ctx.enter_context(tc.psum_pool(name="back", bufs=2))
 
+        zeros = keep.tile([P, WARM_COLUMNS], F32)
+        nc.vector.memset(zeros[:], 0.0)
         ident_f32 = keep.tile([P, P], F32)
         make_identity(nc, ident_f32[:])
         ident_bf16 = keep.tile([P, P], BF16)
@@ -214,9 +217,8 @@ def tile_onebitlinear_s_kernel(
             for first, width in PARTS:
                 if first <= c < first + width:
                     if c == first:
-                        h_part = (front if width == 1 else back).tile(
-                            [P, width, P], F32, name="h_part%d" % first, tag="front" if width == 1 else "back"
-                        )
+                        pool, tag = (back, "back") if first + width < chunks else (front, "front")
+                        h_part = pool.tile([P, width, P], F32, name="h_part%d" % first, tag=tag)
                         h_parts[first] = h_part
                     nc.tensor.transpose(
                         h_parts[first][:, c - first, :], h_cols[:, c, :], ident_f32[:]
@@ -228,9 +230,11 @@ def tile_onebitlinear_s_kernel(
                 out=stats[:, i, :], in_=h_parts[first][:].rearrange("p c q -> p (c q)")
             )
 
-        warm_bank = back.tile([P, P], F32, name="warm_bank", tag="back")
+        warm_bank = back.tile([P, WARM_COLUMNS], F32, name="warm_bank", tag="back")
         for i in range(WARM_UPS):
-            nc.tensor.transpose(warm_bank[:], ident_f32[:], ident_f32[:])
+            nc.tensor.matmul(
+                warm_bank[:], lhsT=zeros[:, 0:P], rhs=zeros[:], start=True, stop=True
+            )
 
         transpose_weights(0)
         leave(0)
@@ -238,43 +242,40 @@ def tile_onebitlinear_s_kernel(
         leave(1)
         transpose_weights(2)
         leave(2)
-        x_bank = work.tile([P, HALVES, passes, P], F32, tag="work")
-        transpose_words(x_sb, x_bank)
         quantise_weights(0)
         double_on_vector(1)
+        transpose_weights(3)
+        leave(3)
+        x_bank = work.tile([P, HALVES, passes, P], F32, tag="work")
+        transpose_words(x_sb, x_bank)
+        quantise_weights(1)
         nc.vector.tensor_tensor(
             out=grouped_view(xs[:]),
             in0=as_grouped(x_bank),
             in1=ics_cols[:].unsqueeze(2).to_broadcast([P, passes, P, HALVES, PAIR]),
             op=ALU.mult,
         )
-        transpose_weights(3)
-        leave(3)
-        quantise_weights(1)
-        nc.vector.quantize_mx(out=x_codes[:].bitcast(FP8X4), scales=x_scales[:], in_=xs[:])
         vec_bank = work.tile([P, P], BF16, tag="work")
         nc.tensor.transpose(vec_bank[:], vec_rows[:], ident_bf16[:])
+        transpose_weights(4)
+        leave(4)
+        quantise_weights(2)
+        nc.vector.quantize_mx(out=x_codes[:].bitcast(FP8X4), scales=x_scales[:], in_=xs[:])
         chan_cols = keep.tile([P, 2 * chunks], F32)
         nc.vector.tensor_copy(out=chan_cols[:], in_=vec_bank[:, 0 : 2 * chunks])
         beta_cols = keep.tile([P, chunks], BF16)
         nc.vector.tensor_copy(out=beta_cols[:], in_=vec_bank[:, 2 * chunks : 3 * chunks])
-        transpose_weights(4)
-        leave(4)
-        quantise_weights(2)
         transpose_weights(5)
         leave(5)
         quantise_weights(3)
         double_on_vector(5)
         transpose_weights(6)
         leave(6)
-        multiply(0)
-        multiply(1)
-        multiply(2)
         transpose_weights(7)
         leave(7, passes)
         quantise_weights(4)
-        multiply(3)
-        multiply(4)
+        for c in range(5):
+            multiply(c)
         quantise_weights(5)
         multiply(5)
         scale(0)
@@ -298,6 +299,7 @@ def tile_onebitlinear_s_kernel(
         transpose_back(4)
         transpose_back(5)
         transpose_back(6)
+        measure(1)
         scale(7)
         transpose_back(7)
         beta_rows = front.tile([P, chunks, P], BF16, name="beta_rows", tag="front")
@@ -305,7 +307,6 @@ def tile_onebitlinear_s_kernel(
             nc.tensor.transpose(
                 beta_rows[:, c, :], beta_cols[:, c : c + 1].to_broadcast([P, P]), ident_bf16[:]
             )
-        measure(1)
         measure(2)
 
         mean_var = keep.tile([P, 2], F32)

from contextlib import ExitStack

import concourse.mybir as mybir
from concourse.masks import make_identity

BF16 = mybir.dt.bfloat16
F32 = mybir.dt.float32
U32 = mybir.dt.uint32
U8 = mybir.dt.uint8
FP8X4 = mybir.dt.float8_e4m3fn_x4
ALU = mybir.AluOpType
ACT = mybir.ActivationFunctionType

P = 128
PACK = 4
K_PASS = P * PACK
PAIR = 2
HALVES = PACK // PAIR
STATS = 6
LN_EPS = 1e-5

SIGN_SCALE = 2.0**20
SIGN_BIAS = 2.0**-120

VECTOR_CHUNKS = (1, 5)
X_CHUNK = 4

BANKS_OF_PRODUCTS = {0: 2, 2: 2, 4: 3, 7: 1}
SCALAR_SCALES = 4
WARM_UPS = 2
WARM_COLUMNS = 256

PARTS = ((0, 4), (4, 2), (6, 2))

FLOPS = 2 * 128 * 1024 * 1024


def tile_onebitlinear_s_kernel(
    tc, x, weight, in_channel_scale, out_channel_scale, bias, ln_gamma, ln_beta, out
):
    nc = tc.nc
    x_rows = x.flatten_outer_dims()
    out_rows = out.flatten_outer_dims()
    d_out, d_in = weight.shape
    assert x_rows.shape[0] == P
    passes = d_in // K_PASS
    chunks = d_out // P

    with ExitStack() as ctx:
        ctx.enter_context(tc.manual_schedule())
        keep = ctx.enter_context(tc.tile_pool(name="keep", bufs=1))
        loads = ctx.enter_context(tc.tile_pool(name="loads", bufs=chunks))
        signs = ctx.enter_context(tc.tile_pool(name="signs", bufs=chunks))
        front = ctx.enter_context(tc.psum_pool(name="front", bufs=4))
        work = ctx.enter_context(tc.psum_pool(name="work", bufs=2))
        back = ctx.enter_context(tc.psum_pool(name="back", bufs=2))

        zeros = keep.tile([P, WARM_COLUMNS], F32)
        nc.vector.memset(zeros[:], 0.0)
        ident_f32 = keep.tile([P, P], F32)
        make_identity(nc, ident_f32[:])
        ident_bf16 = keep.tile([P, P], BF16)
        make_identity(nc, ident_bf16[:])
        vec_rows = keep.tile([P, P], BF16)
        nc.vector.memset(vec_rows[:], 0.0)
        eps_col = keep.tile([P, 1], F32)
        nc.vector.memset(eps_col[:], LN_EPS)
        sign_bias_col = keep.tile([P, 1], F32)
        nc.vector.memset(sign_bias_col[:], SIGN_BIAS)

        ics_cols = keep.tile([P, passes, HALVES, PAIR], BF16)
        with nc.allow_non_contiguous_dma(reason="512 pieces of 4 bytes, once"):
            nc.scalar.dma_start(
                out=ics_cols[:],
                in_=in_channel_scale.rearrange(
                    "(g u p e) -> p g u e", g=passes, u=HALVES, e=PAIR
                ),
            )
        for v, vector in enumerate((out_channel_scale, bias, ln_beta)):
            nc.scalar.dma_start(
                out=vec_rows[v * chunks : (v + 1) * chunks, :],
                in_=vector.rearrange("(c p) -> c p", p=P),
            )
        warm = keep.tile([P, 1], F32)
        nc.scalar.activation(out=warm[:], in_=eps_col[:], func=ACT.Sqrt)

        w_by_chunk = weight.rearrange("(c p) k -> c p k", p=P)
        x_sb = keep.tile([P, d_in], BF16)
        w_chunks = []
        for c in range(chunks):
            if c == X_CHUNK:
                nc.sync.dma_start(out=x_sb[:], in_=x_rows)
            w_chunk = loads.tile([P, d_in], BF16)
            pieces = passes if c == 0 else 1
            for i in range(pieces):
                cols = slice(i * d_in // pieces, (i + 1) * d_in // pieces)
                nc.sync.dma_start(out=w_chunk[:, cols], in_=w_by_chunk[c][:, cols])
            w_chunks.append(w_chunk)
        gamma_rows = keep.tile([P, d_out], BF16)
        nc.sync.dma_start(out=gamma_rows[:], in_=ln_gamma.partition_broadcast(P))

        def transpose_words(src, bank):
            words = src[:].bitcast(F32)
            for g in range(passes):
                for u in range(HALVES):
                    first = (g * HALVES + u) * P
                    nc.tensor.transpose(
                        bank[:, u, g, :], words[:, first : first + P], ident_f32[:]
                    )

        def as_grouped(bank):
            return bank[:].bitcast(BF16).rearrange("p u g (r e) -> p g r u e", e=PAIR)

        def grouped_view(tile_ap):
            return tile_ap.rearrange(
                "p (g r u e) -> p g r u e", g=passes, u=HALVES, e=PAIR
            )

        w_banks = {}
        w_signs = {}
        products = {}
        w_codes = keep.tile([P, chunks, passes * P], U32, align_bytes=64)
        w_scales = keep.tile([P, chunks, passes * P], U8, align_bytes=64)
        x_codes = keep.tile([P, passes * P], U32, align_bytes=64)
        x_scales = keep.tile([P, passes * P], U8, align_bytes=64)
        xs = keep.tile([P, passes * P * PACK], BF16, align_bytes=64)
        h_cols = keep.tile([P, chunks, P], F32)
        stats = keep.tile([P, len(PARTS), STATS], F32)
        h_parts = {}
        both = slice(0, passes)

        def transpose_weights(c):
            w_bank = front.tile([P, HALVES, passes, P], F32, tag="front")
            transpose_words(w_chunks[c], w_bank)
            w_banks[c] = w_bank
            w_sign = signs.tile([P, passes * P * PACK], BF16, align_bytes=64)
            w_signs[c] = w_sign

        def sign_on_scalar(c, pieces=1):
            for i in range(pieces):
                held = slice(i * passes // pieces, (i + 1) * passes // pieces)
                nc.scalar.activation(
                    out=grouped_view(w_signs[c][:])[:, held],
                    in_=as_grouped(w_banks[c])[:, held],
                    func=ACT.Sign,
                    bias=sign_bias_col[:],
                    scale=SIGN_SCALE,
                )

        def compare_on_vector(c):
            nc.vector.tensor_scalar(
                out=grouped_view(w_signs[c][:]),
                in0=as_grouped(w_banks[c]),
                scalar1=0.0,
                scalar2=0.5,
                op0=ALU.is_ge,
                op1=ALU.subtract,
            )

        def double_on_vector(c):
            nc.vector.tensor_scalar_mul(out=w_signs[c][:], in0=w_signs[c][:], scalar1=2.0)

        def leave(c, pieces=1):
            if c in VECTOR_CHUNKS:
                compare_on_vector(c)
            else:
                sign_on_scalar(c, pieces)

        def quantise_weights(c, gs=both):
            cols = slice(gs.start * P, gs.stop * P)
            nc.vector.quantize_mx(
                out=w_codes[:, c, cols].bitcast(FP8X4),
                scales=w_scales[:, c, cols],
                in_=w_signs[c][:, gs.start * P * PACK : gs.stop * P * PACK],
            )

        def multiply(c, gs=both):
            if c in BANKS_OF_PRODUCTS and gs.start == 0:
                held = BANKS_OF_PRODUCTS[c]
                pool, tag = (front, "front") if held > 2 else (work, "work")
                bank = pool.tile([P, held, P], F32, name="products%d" % c, tag=tag)
                for i in range(held):
                    products[c + i] = bank[:, i, :]
            for g in range(gs.start, gs.stop):
                cols = slice(g * P, (g + 1) * P)
                nc.tensor.matmul_mx(
                    out=products[c],
                    lhsT=w_codes[:, c, cols].bitcast(FP8X4),
                    lhsT_scale=w_scales[:, c, cols],
                    rhs=x_codes[:, cols].bitcast(FP8X4),
                    rhs_scale=x_scales[:, cols],
                    start=(g == 0),
                    stop=(g == passes - 1),
                )

        def scale(c):
            scale_col = chan_cols[:, c : c + 1]
            bias_col = chan_cols[:, chunks + c : chunks + c + 1]
            if c >= SCALAR_SCALES:
                nc.scalar.activation(
                    out=h_cols[:, c, :],
                    in_=products[c],
                    func=ACT.Identity,
                    bias=bias_col,
                    scale=scale_col,
                )
            else:
                nc.vector.tensor_scalar(
                    out=h_cols[:, c, :],
                    in0=products[c],
                    scalar1=scale_col,
                    scalar2=bias_col,
                    op0=ALU.mult,
                    op1=ALU.add,
                )
        def transpose_back(c):
            for first, width in PARTS:
                if first <= c < first + width:
                    if c == first:
                        pool, tag = (back, "back") if first + width < chunks else (front, "front")
                        h_part = pool.tile([P, width, P], F32, name="h_part%d" % first, tag=tag)
                        h_parts[first] = h_part
                    nc.tensor.transpose(
                        h_parts[first][:, c - first, :], h_cols[:, c, :], ident_f32[:]
                    )

        def measure(i):
            first, width = PARTS[i]
            nc.vector.bn_stats(
                out=stats[:, i, :], in_=h_parts[first][:].rearrange("p c q -> p (c q)")
            )

        warm_bank = back.tile([P, WARM_COLUMNS], F32, name="warm_bank", tag="back")
        for i in range(WARM_UPS):
            nc.tensor.matmul(
                warm_bank[:], lhsT=zeros[:, 0:P], rhs=zeros[:], start=True, stop=True
            )

        transpose_weights(0)
        leave(0)
        transpose_weights(1)
        leave(1)
        transpose_weights(2)
        leave(2)
        quantise_weights(0)
        double_on_vector(1)
        transpose_weights(3)
        leave(3)
        x_bank = work.tile([P, HALVES, passes, P], F32, tag="work")
        transpose_words(x_sb, x_bank)
        quantise_weights(1)
        nc.vector.tensor_tensor(
            out=grouped_view(xs[:]),
            in0=as_grouped(x_bank),
            in1=ics_cols[:].unsqueeze(2).to_broadcast([P, passes, P, HALVES, PAIR]),
            op=ALU.mult,
        )
        vec_bank = work.tile([P, P], BF16, tag="work")
        nc.tensor.transpose(vec_bank[:], vec_rows[:], ident_bf16[:])
        transpose_weights(4)
        leave(4)
        quantise_weights(2)
        nc.vector.quantize_mx(out=x_codes[:].bitcast(FP8X4), scales=x_scales[:], in_=xs[:])
        chan_cols = keep.tile([P, 2 * chunks], F32)
        nc.vector.tensor_copy(out=chan_cols[:], in_=vec_bank[:, 0 : 2 * chunks])
        beta_cols = keep.tile([P, chunks], BF16)
        nc.vector.tensor_copy(out=beta_cols[:], in_=vec_bank[:, 2 * chunks : 3 * chunks])
        transpose_weights(5)
        leave(5)
        quantise_weights(3)
        double_on_vector(5)
        transpose_weights(6)
        leave(6)
        transpose_weights(7)
        leave(7, passes)
        quantise_weights(4)
        for c in range(5):
            multiply(c)
        quantise_weights(5)
        multiply(5)
        scale(0)
        scale(1)
        transpose_back(0)
        transpose_back(1)
        quantise_weights(6)
        multiply(6)
        scale(2)
        scale(3)
        transpose_back(2)
        transpose_back(3)
        quantise_weights(7, slice(0, 1))
        multiply(7, slice(0, 1))
        scale(4)
        scale(5)
        scale(6)
        quantise_weights(7, slice(1, passes))
        multiply(7, slice(1, passes))
        measure(0)
        transpose_back(4)
        transpose_back(5)
        transpose_back(6)
        measure(1)
        scale(7)
        transpose_back(7)
        beta_rows = front.tile([P, chunks, P], BF16, name="beta_rows", tag="front")
        for c in range(chunks):
            nc.tensor.transpose(
                beta_rows[:, c, :], beta_cols[:, c : c + 1].to_broadcast([P, P]), ident_bf16[:]
            )
        measure(2)

        mean_var = keep.tile([P, 2], F32)
        nc.vector.bn_aggr(out=mean_var[:], in_=stats[:].rearrange("p c s -> p (c s)"))
        std = keep.tile([P, 1], F32)
        nc.scalar.activation(out=std[:], in_=mean_var[:, 1:2], func=ACT.Sqrt, bias=eps_col[:])
        rstd = keep.tile([P, 1], F32)
        centred = keep.tile([P, d_out], F32)
        for first, width in PARTS:
            cols = slice(first * P, (first + width) * P)
            nc.vector.scalar_tensor_tensor(
                out=centred[:, cols],
                in0=h_parts[first][:].rearrange("p c q -> p (c q)"),
                scalar=mean_var[:, 0:1],
                in1=gamma_rows[:, cols],
                op0=ALU.subtract,
                op1=ALU.mult,
            )
            if first == 0:
                nc.vector.reciprocal(out=rstd[:], in_=std[:])
        result = keep.tile([P, d_out], F32)
        for first, width in PARTS:
            cols = slice(first * P, (first + width) * P)
            nc.vector.scalar_tensor_tensor(
                out=result[:, cols],
                in0=centred[:, cols],
                scalar=rstd[:],
                in1=beta_rows[:].rearrange("p c q -> p (c q)")[:, cols],
                op0=ALU.mult,
                op1=ALU.add,
            )
            nc.sync.dma_start(out=out_rows[:, cols], in_=result[:, cols])
